import numpy as np
import ml_dtypes


def mxq(x, axis, fmt="e4m3"):
    dtype, down = {"e4m3": (ml_dtypes.float8_e4m3fn, 7), "e5m2": (ml_dtypes.float8_e5m2, 14)}[fmt]
    v = np.moveaxis(np.asarray(x, np.float32).astype(ml_dtypes.bfloat16).astype(np.float64), axis, -1)
    blocks = v.reshape(v.shape[:-1] + (-1, 32))
    amax = np.abs(blocks).max(-1, keepdims=True)
    byte = np.maximum(np.where(amax > 0, np.frexp(amax)[1] - 1 + 127, 0) - down, 1)
    scale = np.exp2(byte - 127.0)
    codes = (blocks / scale).astype(np.float32).astype(dtype).astype(np.float64)
    return np.moveaxis((codes * scale).reshape(v.shape), -1, axis)


WIDE = False


def mx_kscale(k):
    if not WIDE:
        return np.ones(k)
    levels = np.array([10, -10, 5, -5, 0])
    a = np.random.permutation(np.resize(levels, k // 512 * 4)).reshape(k // 512, 4)
    idx = np.arange(k)
    return np.exp2(a[idx // 512, idx % 128 // 32])


BF16 = ml_dtypes.bfloat16


def bf(x):
    return np.asarray(x, np.float32).astype(BF16)


def f64(x):
    return np.asarray(x).astype(np.float64)


E2M1 = np.array([0.0, 0.5, 1.0, 1.5, 2.0, 3.0, 4.0, 6.0, -0.0, -0.5, -1.0, -1.5, -2.0, -3.0, -4.0, -6.0])


def pack_weight(w, fmt):
    k, n = w.shape
    w = f64(bf(w)).reshape(k // 32, 32, n)
    amax = np.abs(w).max(1)
    if fmt == "e4m3":
        byte = np.frexp(amax)[1] - 1 + 127 - 7
    else:
        mant, ex = np.frexp(amax / 6.0)
        byte = np.where(mant > 0.5, ex, ex - 1) + 127
    byte = np.clip(np.where(amax > 0, byte, 1), 1, 254)
    scaled = (w * np.exp2(127.0 - byte)[:, None, :]).reshape(k, n).astype(np.float32)
    by_word = np.ascontiguousarray(scaled.reshape(k // 512, 128, 4, n).transpose(0, 1, 3, 2))
    if fmt == "e4m3":
        words = by_word.astype(ml_dtypes.float8_e4m3fn).view(np.uint8)
    else:
        c = by_word.astype(ml_dtypes.float4_e2m1fn).view(np.uint8) & 0xF
        words = c[..., 0::2] | (c[..., 1::2] << 4)
    return np.ascontiguousarray(words), np.ascontiguousarray(byte.astype(np.uint8).reshape(k // 512, 16, n))


def unpack_weight(words, scales, fmt):
    g, p, n, _ = words.shape
    if fmt == "e4m3":
        vals = np.ascontiguousarray(words).view(ml_dtypes.float8_e4m3fn).astype(np.float64)
    else:
        nib = np.empty((g, p, n, 4), np.uint8)
        nib[..., 0::2] = words & 0xF
        nib[..., 1::2] = words >> 4
        vals = E2M1[nib]
    vals = vals * np.repeat(np.exp2(scales.astype(np.float64) - 127.0), 8, axis=1)[..., None]
    return vals.transpose(0, 1, 3, 2).reshape(g * 512, n)


B, S, D, HD, M = 4, 1024, 2048, 128, 4
N = S // M
NEG = float(np.finfo(np.float32).min)
FMT = "e4m3"


def prev(x):
    return np.concatenate([np.zeros_like(x[:, :1]), x[:, :-1]], axis=1)


def setup_inputs():
    s = mx_kscale(D)

    def w():
        return pack_weight(np.random.standard_normal((D, HD)) / np.sqrt(D) / s[:, None], FMT)

    h = bf(np.random.standard_normal((B, S, D)) * s)
    w_kv_a_words, w_kv_a_scales = w()
    w_kv_b_words, w_kv_b_scales = w()
    w_z_a_words, w_z_a_scales = w()
    w_z_b_words, w_z_b_scales = w()
    b_a = bf(np.random.standard_normal((M, HD)) * 0.5)
    b_b = bf(np.random.standard_normal((M, HD)) * 0.5)
    return {"h": h,
            "w_kv_a_words": w_kv_a_words, "w_kv_a_scales": w_kv_a_scales,
            "w_kv_b_words": w_kv_b_words, "w_kv_b_scales": w_kv_b_scales,
            "w_z_a_words": w_z_a_words, "w_z_a_scales": w_z_a_scales,
            "w_z_b_words": w_z_b_words, "w_z_b_scales": w_z_b_scales,
            "b_a": b_a,
            "b_b": b_b}


def reference(h, w_kv_a_words, w_kv_a_scales, w_kv_b_words, w_kv_b_scales, w_z_a_words, w_z_a_scales, w_z_b_words, w_z_b_scales, b_a, b_b):
    hq = mxq(f64(h), 2, "e4m3")
    c_a = (hq @ unpack_weight(w_kv_a_words, w_kv_a_scales, FMT)).reshape(B, N, M, HD)
    c_b = (hq @ unpack_weight(w_kv_b_words, w_kv_b_scales, FMT)).reshape(B, N, M, HD)
    z_a = (hq @ unpack_weight(w_z_a_words, w_z_a_scales, FMT)).reshape(B, N, M, HD)
    z_b = (hq @ unpack_weight(w_z_b_words, w_z_b_scales, FMT)).reshape(B, N, M, HD)
    logits = np.concatenate([prev(z_b) + f64(b_b), z_a + f64(b_a)], axis=2)
    valid = np.concatenate([np.broadcast_to((np.arange(N) > 0)[:, None], (N, M)), np.ones((N, M), bool)], axis=1)
    logits = np.where(valid[None, :, :, None], logits, NEG)
    e = np.exp(logits - logits.max(axis=2, keepdims=True))
    weights = e / e.sum(axis=2, keepdims=True)
    c_vals = np.concatenate([prev(c_b), c_a], axis=2)
    return np.sum(weights * c_vals, axis=2)

@@ -1,0 +1,349 @@
+from contextlib import ExitStack
+
+import concourse.mybir as mybir
+from concourse.masks import make_identity
+
+F32 = mybir.dt.float32
+BF16 = mybir.dt.bfloat16
+I32 = mybir.dt.int32
+U32 = mybir.dt.uint32
+U8 = mybir.dt.uint8
+FP8X4 = mybir.dt.float8_e4m3fn_x4
+ALU = mybir.AluOpType
+ACT = mybir.ActivationFunctionType
+
+P = 128
+SEQS, SEQ_LEN, K, FEATURES, BLOCK = 4, 1024, 2048, 128, 4
+K_PASS = 4 * P
+PASSES = K // K_PASS
+WORDS = K_PASS // 2
+TILE_TOKENS = BLOCK * P
+TILES = SEQS * SEQ_LEN // TILE_TOKENS
+TILES_PER_SEQ = SEQ_LEN // TILE_TOKENS
+PLANE = SEQ_LEN // BLOCK + 8
+NEG = -3.4028234663852886e38
+Z_B, Z_A, C_B, C_A = 0, 1, 2, 3
+B_PLANES, A_PLANES = slice(0, BLOCK), slice(BLOCK, 2 * BLOCK)
+
+FLOPS = 2 * SEQS * SEQ_LEN * K * 4 * FEATURES
+
+
+def tile_tokenlevelcompressor_pa_kernel(
+    tc,
+    h,
+    w_kv_a_words,
+    w_kv_a_scales,
+    w_kv_b_words,
+    w_kv_b_scales,
+    w_z_a_words,
+    w_z_a_scales,
+    w_z_b_words,
+    w_z_b_scales,
+    b_a,
+    b_b,
+    out,
+):
+    nc = tc.nc
+    weights = {
+        Z_B: (w_z_b_words, w_z_b_scales),
+        Z_A: (w_z_a_words, w_z_a_scales),
+        C_B: (w_kv_b_words, w_kv_b_scales),
+        C_A: (w_kv_a_words, w_kv_a_scales),
+    }
+    h_tiles = h.flatten_outer_dims().rearrange("(t p i) k -> t p i k", p=P, i=BLOCK)
+    out_tiles = out.flatten_outer_dims().rearrange("(t p) f -> t p f", p=P)
+
+    with ExitStack() as ctx:
+        const = ctx.enter_context(tc.tile_pool(name="const", bufs=1))
+        h_pool = ctx.enter_context(tc.tile_pool(name="h", bufs=6))
+        grouped_pool = ctx.enter_context(tc.tile_pool(name="grouped", bufs=3))
+        mx_pool = ctx.enter_context(tc.tile_pool(name="mx", bufs=3))
+        seq_pool = ctx.enter_context(tc.tile_pool(name="seq", bufs=2))
+        work = ctx.enter_context(tc.tile_pool(name="work", bufs=2))
+        psum_t = ctx.enter_context(tc.psum_pool(name="psum_t", bufs=4))
+        psum_acc = ctx.enter_context(tc.psum_pool(name="psum_acc", bufs=4))
+
+        h_sb = {}
+        grouped = {}
+        codes = {}
+        scales = {}
+        acc = {}
+        logits = {}
+        values_b = {}
+        part = {}
+
+        ident = const.tile([P, P], F32)
+        w_codes = const.tile([P, 4, PASSES, FEATURES], U32, align_bytes=64)
+        w_scales = const.tile([P, 4, PASSES, FEATURES], U8, align_bytes=64)
+        bias = const.tile([P, 2 * BLOCK], F32)
+
+        def live(t):
+            return 0 <= t < TILES
+
+        def columns_of(t):
+            first = P * (t % TILES_PER_SEQ)
+            return slice(first, first + P)
+
+        def shifted_columns_of(t):
+            first = P * (t % TILES_PER_SEQ) + 1
+            return slice(first, first + P)
+
+        def load_h(t, pair):
+            if not live(t):
+                return
+            h_sb[t, pair] = h_pool.tile([P, 2, K], BF16, name="h_sb")
+            nc.sync.dma_start(out=h_sb[t, pair][:], in_=h_tiles[t][:, 2 * pair : 2 * pair + 2, :])
+
+        def load_codes(a):
+            nc.sync.dma_start(
+                out=w_codes[:, a].bitcast(I32),
+                in_=weights[a][0].rearrange("g p n t -> p g (n t)").bitcast(I32),
+            )
+
+        def load_scales(a):
+            for quadrant in range(4):
+                nc.gpsimd.dma_start(
+                    out=w_scales[32 * quadrant : 32 * quadrant + 4, a].bitcast(F32),
+                    in_=weights[a][1][:, 4 * quadrant : 4 * quadrant + 4, :]
+                    .rearrange("g r n -> r g n")
+                    .bitcast(F32),
+                )
+
+        def load_bias():
+            rows_bf16 = const.tile([P, P], BF16)
+            nc.vector.memset(rows_bf16[:], 0.0)
+            nc.sync.dma_start(out=rows_bf16[0:BLOCK, :], in_=b_b)
+            nc.sync.dma_start(out=rows_bf16[BLOCK : 2 * BLOCK, :], in_=b_a)
+            rows = const.tile([P, P], F32)
+            nc.vector.tensor_copy(out=rows[:], in_=rows_bf16[:])
+            columns = psum_t.tile([P, 2, 2, P], F32, name="bank")
+            nc.tensor.transpose(columns[:, 0, 0, :], rows[:], ident[:])
+            nc.vector.tensor_copy(out=bias[:], in_=columns[:, 0, 0, 0 : 2 * BLOCK])
+
+        def transpose_pair(t, pair):
+            if not live(t):
+                return
+            h_words = h_sb[t, pair][:].bitcast(F32)
+            grouped[t, pair] = grouped_pool.tile(
+                [P, PASSES, 2, P, 4], BF16, name="grouped", align_bytes=64
+            )
+            for g in range(PASSES):
+                bank = psum_t.tile([P, 2, 2, P], F32, name="bank")
+                for i in range(2):
+                    for u in range(2):
+                        nc.tensor.transpose(
+                            bank[:, i, u, :],
+                            h_words[:, i, WORDS * g + u : WORDS * (g + 1) : 2],
+                            ident[:],
+                        )
+                nc.scalar.copy(
+                    out=grouped[t, pair][:, g].bitcast(F32),
+                    in_=bank[:].rearrange("p i u c -> p i c u"),
+                )
+
+        def quantise(t, pair, g):
+            if not live(t):
+                return
+            if (pair, g) == (0, 0):
+                codes[t] = mx_pool.tile([P, PASSES, BLOCK, P], U32, name="codes", align_bytes=64)
+                scales[t] = mx_pool.tile([P, PASSES, BLOCK, P], U8, name="scales", align_bytes=64)
+            tokens = slice(2 * pair, 2 * pair + 2)
+            nc.vector.quantize_mx(
+                out=codes[t][:, g, tokens].rearrange("p i c -> p (i c)").bitcast(FP8X4),
+                scales=scales[t][:, g, tokens].rearrange("p i c -> p (i c)"),
+                in_=grouped[t, pair][:, g].rearrange("p i c t -> p (i c t)"),
+            )
+
+        def project(t, a):
+            if not live(t):
+                return
+            acc[t, a] = psum_acc.tile([P, BLOCK, P], F32, name="acc")
+            for g in range(PASSES):
+                nc.tensor.matmul_mx(
+                    out=acc[t, a][:].rearrange("p i j -> p (i j)"),
+                    lhsT=w_codes[:, a, g, :].bitcast(FP8X4),
+                    lhsT_scale=w_scales[:, a, g, :],
+                    rhs=codes[t][:, g].rearrange("p i c -> p (i c)").bitcast(FP8X4),
+                    rhs_scale=scales[t][:, g].rearrange("p i c -> p (i c)"),
+                    start=(g == 0),
+                    stop=(g == PASSES - 1),
+                )
+
+        def open_sequence(t):
+            if not live(t):
+                return
+            if t % TILES_PER_SEQ != 0:
+                logits[t] = logits[t - 1]
+                values_b[t] = values_b[t - 1]
+                return
+            logits[t] = seq_pool.tile([P, 2 * BLOCK, PLANE], F32, name="logits")
+            values_b[t] = seq_pool.tile([P, BLOCK, PLANE], F32, name="values_b")
+            nc.vector.memset(logits[t][:, 0:BLOCK, 0:8], NEG)
+            nc.vector.memset(values_b[t][:, :, 0:8], 0.0)
+
+        def add_bias(t):
+            if not live(t):
+                return
+            for i in range(BLOCK):
+                nc.scalar.activation(
+                    out=logits[t][:, i, shifted_columns_of(t)],
+                    in_=acc[t, Z_B][:, i, :],
+                    func=ACT.Identity,
+                    bias=bias[:, i : i + 1],
+                )
+            for i in range(BLOCK):
+                nc.scalar.activation(
+                    out=logits[t][:, BLOCK + i, columns_of(t)],
+                    in_=acc[t, Z_A][:, i, :],
+                    func=ACT.Identity,
+                    bias=bias[:, BLOCK + i : BLOCK + i + 1],
+                )
+
+        def max_of_8(t):
+            if not live(t):
+                return
+            mine = logits[t][:, :, columns_of(t)]
+            part[t, "max4"] = work.tile([P, 4, P], F32, name="max4")
+            nc.vector.tensor_max(out=part[t, "max4"][:], in0=mine[:, 0:4], in1=mine[:, 4:8])
+
+        def max_of_4(t):
+            if not live(t):
+                return
+            max4 = part[t, "max4"]
+            part[t, "max2"] = work.tile([P, 2, P], F32, name="max2")
+            nc.vector.tensor_max(out=part[t, "max2"][:], in0=max4[:, 0:2], in1=max4[:, 2:4])
+
+        def max_of_2(t):
+            if not live(t):
+                return
+            max2 = part[t, "max2"]
+            part[t, "max1"] = work.tile([P, P], F32, name="max1")
+            nc.vector.tensor_max(out=part[t, "max1"][:], in0=max2[:, 0], in1=max2[:, 1])
+
+        def subtract_max(t, planes):
+            if not live(t):
+                return
+            if planes == B_PLANES:
+                part[t, "terms"] = work.tile([P, 2, 2 * BLOCK, P], F32, name="terms")
+            nc.vector.tensor_tensor(
+                out=part[t, "terms"][:, 0, planes],
+                in0=logits[t][:, planes, columns_of(t)],
+                in1=part[t, "max1"][:].unsqueeze(1).to_broadcast([P, BLOCK, P]),
+                op=ALU.subtract,
+            )
+
+        def shift_values_b(t):
+            if not live(t):
+                return
+            nc.scalar.copy(out=values_b[t][:, :, shifted_columns_of(t)], in_=acc[t, C_B][:])
+
+        def exponentials(t, planes):
+            if not live(t):
+                return
+            terms = part[t, "terms"]
+            nc.scalar.activation(out=terms[:, 0, planes], in_=terms[:, 0, planes], func=ACT.Exp)
+
+        def products(t, planes):
+            if not live(t):
+                return
+            terms = part[t, "terms"]
+            values = values_b[t][:, :, columns_of(t)] if planes == B_PLANES else acc[t, C_A][:]
+            nc.vector.tensor_mul(out=terms[:, 1, planes], in0=terms[:, 0, planes], in1=values)
+
+        def sum_of_8(t):
+            if not live(t):
+                return
+            terms = part[t, "terms"]
+            part[t, "sum4"] = work.tile([P, 2, 4, P], F32, name="sum4")
+            nc.vector.tensor_add(out=part[t, "sum4"][:], in0=terms[:, :, 0:4], in1=terms[:, :, 4:8])
+
+        def sum_of_4(t):
+            if not live(t):
+                return
+            sum4 = part[t, "sum4"]
+            part[t, "sum2"] = work.tile([P, 2, 2, P], F32, name="sum2")
+            nc.vector.tensor_add(out=part[t, "sum2"][:], in0=sum4[:, :, 0:2], in1=sum4[:, :, 2:4])
+
+        def sum_of_2(t):
+            if not live(t):
+                return
+            sum2 = part[t, "sum2"]
+            part[t, "sum1"] = work.tile([P, 2, P], F32, name="sum1")
+            nc.vector.tensor_add(out=part[t, "sum1"][:], in0=sum2[:, :, 0], in1=sum2[:, :, 1])
+
+        def invert(t):
+            if not live(t):
+                return
+            part[t, "inverse"] = work.tile([P, P], F32, name="inverse")
+            nc.vector.reciprocal(out=part[t, "inverse"][:], in_=part[t, "sum1"][:, 0])
+
+        def normalise(t):
+            if not live(t):
+                return
+            part[t, "result"] = work.tile([P, P], F32, name="result")
+            nc.vector.tensor_mul(
+                out=part[t, "result"][:], in0=part[t, "sum1"][:, 1], in1=part[t, "inverse"][:]
+            )
+
+        def store(t):
+            if not live(t):
+                return
+            bank = psum_t.tile([P, 2, 2, P], F32, name="bank")
+            nc.tensor.transpose(bank[:, 0, 0, :], part[t, "result"][:], ident[:])
+            rows = work.tile([P, FEATURES], F32, name="out_rows")
+            nc.scalar.copy(out=rows[:], in_=bank[:, 0, 0, :])
+            nc.scalar.dma_start(out=out_tiles[t], in_=rows[:])
+
+        with tc.manual_schedule():
+            nc.vector.memset(w_scales[:].rearrange("p a g n -> p (a g n)").bitcast(I32), 0)
+            make_identity(nc, ident[:])
+            load_bias()
+            load_h(0, 0)
+            load_h(0, 1)
+            load_codes(Z_B)
+            load_codes(Z_A)
+            load_h(1, 0)
+            load_codes(C_B)
+            load_codes(C_A)
+            load_h(1, 1)
+            for a in (Z_B, Z_A, C_B, C_A):
+                load_scales(a)
+
+            for s in range(TILES + 3):
+                load_h(s + 2, 0)
+                load_h(s + 2, 1)
+                open_sequence(s - 1)
+                store(s - 3)
+                transpose_pair(s, 0)
+                project(s - 1, Z_B)
+                project(s - 1, Z_A)
+                add_bias(s - 1)
+
+                products(s - 2, B_PLANES)
+                products(s - 2, A_PLANES)
+                sum_of_8(s - 2)
+                quantise(s, 0, 0)
+                sum_of_4(s - 2)
+                quantise(s, 0, 1)
+                sum_of_2(s - 2)
+                quantise(s, 0, 2)
+                invert(s - 2)
+                quantise(s, 0, 3)
+                normalise(s - 2)
+
+                transpose_pair(s, 1)
+                project(s - 1, C_B)
+                project(s - 1, C_A)
+
+                max_of_8(s - 1)
+                quantise(s, 1, 0)
+                max_of_4(s - 1)
+                quantise(s, 1, 1)
+                max_of_2(s - 1)
+                quantise(s, 1, 2)
+                subtract_max(s - 1, B_PLANES)
+                subtract_max(s - 1, A_PLANES)
+                quantise(s, 1, 3)
+                shift_values_b(s - 1)
+                exponentials(s - 1, B_PLANES)
+                exponentials(s - 1, A_PLANES)

@@ -55,8 +55,8 @@ def tile_tokenlevelcompressor_pa_kernel(
 
     with ExitStack() as ctx:
         const = ctx.enter_context(tc.tile_pool(name="const", bufs=1))
-        h_pool = ctx.enter_context(tc.tile_pool(name="h", bufs=6))
-        grouped_pool = ctx.enter_context(tc.tile_pool(name="grouped", bufs=3))
+        h_pool = ctx.enter_context(tc.tile_pool(name="h", bufs=12))
+        grouped_pool = ctx.enter_context(tc.tile_pool(name="grouped", bufs=8))
         mx_pool = ctx.enter_context(tc.tile_pool(name="mx", bufs=3))
         seq_pool = ctx.enter_context(tc.tile_pool(name="seq", bufs=2))
         work = ctx.enter_context(tc.tile_pool(name="work", bufs=2))
@@ -88,11 +88,14 @@ def tile_tokenlevelcompressor_pa_kernel(
             first = P * (t % TILES_PER_SEQ) + 1
             return slice(first, first + P)
 
-        def load_h(t, pair):
+        def load_h(t, pair, half):
             if not live(t):
                 return
-            h_sb[t, pair] = h_pool.tile([P, 2, K], BF16, name="h_sb")
-            nc.sync.dma_start(out=h_sb[t, pair][:], in_=h_tiles[t][:, 2 * pair : 2 * pair + 2, :])
+            h_sb[t, pair, half] = h_pool.tile([P, 2, K // 2], BF16, name="h_sb")
+            nc.sync.dma_start(
+                out=h_sb[t, pair, half][:],
+                in_=h_tiles[t][:, 2 * pair : 2 * pair + 2, (K // 2) * half : (K // 2) * (half + 1)],
+            )
 
         def load_codes(a):
             nc.sync.dma_start(
@@ -120,14 +123,11 @@ def tile_tokenlevelcompressor_pa_kernel(
             nc.tensor.transpose(columns[:, 0, 0, :], rows[:], ident[:])
             nc.vector.tensor_copy(out=bias[:], in_=columns[:, 0, 0, 0 : 2 * BLOCK])
 
-        def transpose_pair(t, pair):
+        def transpose_quarter(t, pair, half):
             if not live(t):
                 return
-            h_words = h_sb[t, pair][:].bitcast(F32)
-            grouped[t, pair] = grouped_pool.tile(
-                [P, PASSES, 2, P, 4], BF16, name="grouped", align_bytes=64
-            )
-            for g in range(PASSES):
+            h_words = h_sb[t, pair, half][:].bitcast(F32)
+            for g in range(PASSES // 2):
                 bank = psum_t.tile([P, 2, 2, P], F32, name="bank")
                 for i in range(2):
                     for u in range(2):
@@ -136,9 +136,10 @@ def tile_tokenlevelcompressor_pa_kernel(
                             h_words[:, i, WORDS * g + u : WORDS * (g + 1) : 2],
                             ident[:],
                         )
+                tile_g = grouped_pool.tile([P, 2, P, 4], BF16, name="grouped", align_bytes=64)
+                grouped[t, pair, (PASSES // 2) * half + g] = tile_g
                 nc.scalar.copy(
-                    out=grouped[t, pair][:, g].bitcast(F32),
-                    in_=bank[:].rearrange("p i u c -> p i c u"),
+                    out=tile_g[:].bitcast(F32), in_=bank[:].rearrange("p i u c -> p i c u")
                 )
 
         def quantise(t, pair, g):
@@ -151,7 +152,7 @@ def tile_tokenlevelcompressor_pa_kernel(
             nc.vector.quantize_mx(
                 out=codes[t][:, g, tokens].rearrange("p i c -> p (i c)").bitcast(FP8X4),
                 scales=scales[t][:, g, tokens].rearrange("p i c -> p (i c)"),
-                in_=grouped[t, pair][:, g].rearrange("p i c t -> p (i c t)"),
+                in_=grouped[t, pair, g][:].rearrange("p i c t -> p (i c t)"),
             )
 
         def project(t, a):
@@ -181,7 +182,7 @@ def tile_tokenlevelcompressor_pa_kernel(
             nc.vector.memset(logits[t][:, 0:BLOCK, 0:8], NEG)
             nc.vector.memset(values_b[t][:, :, 0:8], 0.0)
 
-        def add_bias(t):
+        def add_bias_b(t):
             if not live(t):
                 return
             for i in range(BLOCK):
@@ -191,6 +192,10 @@ def tile_tokenlevelcompressor_pa_kernel(
                     func=ACT.Identity,
                     bias=bias[:, i : i + 1],
                 )
+
+        def add_bias_a(t):
+            if not live(t):
+                return
             for i in range(BLOCK):
                 nc.scalar.activation(
                     out=logits[t][:, BLOCK + i, columns_of(t)],
@@ -298,26 +303,33 @@ def tile_tokenlevelcompressor_pa_kernel(
             nc.vector.memset(w_scales[:].rearrange("p a g n -> p (a g n)").bitcast(I32), 0)
             make_identity(nc, ident[:])
             load_bias()
-            load_h(0, 0)
-            load_h(0, 1)
+            load_h(0, 0, 0)
+            load_h(0, 0, 1)
+            load_h(0, 1, 0)
+            load_h(0, 1, 1)
             load_codes(Z_B)
             load_codes(Z_A)
-            load_h(1, 0)
+            load_h(1, 0, 0)
+            load_h(1, 0, 1)
             load_codes(C_B)
             load_codes(C_A)
-            load_h(1, 1)
+            load_h(1, 1, 0)
+            load_h(1, 1, 1)
             for a in (Z_B, Z_A, C_B, C_A):
                 load_scales(a)
 
             for s in range(TILES + 3):
-                load_h(s + 2, 0)
-                load_h(s + 2, 1)
+                for pair in range(2):
+                    for half in range(2):
+                        load_h(s + 2, pair, half)
                 open_sequence(s - 1)
                 store(s - 3)
-                transpose_pair(s, 0)
+                transpose_quarter(s, 0, 0)
                 project(s - 1, Z_B)
+                add_bias_b(s - 1)
+                transpose_quarter(s, 0, 1)
                 project(s - 1, Z_A)
-                add_bias(s - 1)
+                add_bias_a(s - 1)
 
                 products(s - 2, B_PLANES)
                 products(s - 2, A_PLANES)
@@ -331,8 +343,10 @@ def tile_tokenlevelcompressor_pa_kernel(
                 quantise(s, 0, 3)
                 normalise(s - 2)
 
-                transpose_pair(s, 1)
+                transpose_quarter(s, 1, 0)
                 project(s - 1, C_B)
+                shift_values_b(s - 1)
+                transpose_quarter(s, 1, 1)
                 project(s - 1, C_A)
 
                 max_of_8(s - 1)
@@ -340,10 +354,9 @@ def tile_tokenlevelcompressor_pa_kernel(
                 max_of_4(s - 1)
                 quantise(s, 1, 1)
                 max_of_2(s - 1)
-                quantise(s, 1, 2)
                 subtract_max(s - 1, B_PLANES)
                 subtract_max(s - 1, A_PLANES)
+                quantise(s, 1, 2)
                 quantise(s, 1, 3)
-                shift_values_b(s - 1)
                 exponentials(s - 1, B_PLANES)
                 exponentials(s - 1, A_PLANES)

@@ -25,6 +25,7 @@ NEG = -3.4028234663852886e38
 Z_B, Z_A, C_B, C_A = 0, 1, 2, 3
 B_PLANES, A_PLANES = slice(0, BLOCK), slice(BLOCK, 2 * BLOCK)
 
+PLANES_LEFT, PLANES_LEFT_AT_THE_END, TILES_AT_THE_END = 2, 8, 2
 FLOPS = 2 * SEQS * SEQ_LEN * K * 4 * FEATURES
 
 
@@ -56,7 +57,7 @@ def tile_tokenlevelcompressor_pa_kernel(
     with ExitStack() as ctx:
         const = ctx.enter_context(tc.tile_pool(name="const", bufs=1))
         h_pool = ctx.enter_context(tc.tile_pool(name="h", bufs=12))
-        grouped_pool = ctx.enter_context(tc.tile_pool(name="grouped", bufs=8))
+        grouped_pool = ctx.enter_context(tc.tile_pool(name="grouped", bufs=4))
         mx_pool = ctx.enter_context(tc.tile_pool(name="mx", bufs=3))
         seq_pool = ctx.enter_context(tc.tile_pool(name="seq", bufs=2))
         work = ctx.enter_context(tc.tile_pool(name="work", bufs=2))
@@ -123,36 +124,34 @@ def tile_tokenlevelcompressor_pa_kernel(
             nc.tensor.transpose(columns[:, 0, 0, :], rows[:], ident[:])
             nc.vector.tensor_copy(out=bias[:], in_=columns[:, 0, 0, 0 : 2 * BLOCK])
 
-        def transpose_quarter(t, pair, half):
+        def transpose_pass(t, g):
             if not live(t):
                 return
-            h_words = h_sb[t, pair, half][:].bitcast(F32)
-            for g in range(PASSES // 2):
+            grouped[t, g] = grouped_pool.tile([P, BLOCK, P, 4], BF16, name="grouped", align_bytes=64)
+            for pair in range(2):
+                h_words = h_sb[t, pair, g // 2][:].bitcast(F32)
+                first = WORDS * (g % 2)
                 bank = psum_t.tile([P, 2, 2, P], F32, name="bank")
                 for i in range(2):
                     for u in range(2):
                         nc.tensor.transpose(
-                            bank[:, i, u, :],
-                            h_words[:, i, WORDS * g + u : WORDS * (g + 1) : 2],
-                            ident[:],
+                            bank[:, i, u, :], h_words[:, i, first + u : first + WORDS : 2], ident[:]
                         )
-                tile_g = grouped_pool.tile([P, 2, P, 4], BF16, name="grouped", align_bytes=64)
-                grouped[t, pair, (PASSES // 2) * half + g] = tile_g
                 nc.scalar.copy(
-                    out=tile_g[:].bitcast(F32), in_=bank[:].rearrange("p i u c -> p i c u")
+                    out=grouped[t, g][:, 2 * pair : 2 * pair + 2].bitcast(F32),
+                    in_=bank[:].rearrange("p i u c -> p i c u"),
                 )
 
-        def quantise(t, pair, g):
+        def quantise(t, g):
             if not live(t):
                 return
-            if (pair, g) == (0, 0):
+            if g == 0:
                 codes[t] = mx_pool.tile([P, PASSES, BLOCK, P], U32, name="codes", align_bytes=64)
                 scales[t] = mx_pool.tile([P, PASSES, BLOCK, P], U8, name="scales", align_bytes=64)
-            tokens = slice(2 * pair, 2 * pair + 2)
             nc.vector.quantize_mx(
-                out=codes[t][:, g, tokens].rearrange("p i c -> p (i c)").bitcast(FP8X4),
-                scales=scales[t][:, g, tokens].rearrange("p i c -> p (i c)"),
-                in_=grouped[t, pair, g][:].rearrange("p i c t -> p (i c t)"),
+                out=codes[t][:, g].rearrange("p i c -> p (i c)").bitcast(FP8X4),
+                scales=scales[t][:, g].rearrange("p i c -> p (i c)"),
+                in_=grouped[t, g][:].rearrange("p i c t -> p (i c t)"),
             )
 
         def project(t, a):
@@ -229,9 +228,9 @@ def tile_tokenlevelcompressor_pa_kernel(
             if not live(t):
                 return
             if planes == B_PLANES:
-                part[t, "terms"] = work.tile([P, 2, 2 * BLOCK, P], F32, name="terms")
+                part[t, 8] = work.tile([P, 2, 2 * BLOCK, P], F32, name="terms")
             nc.vector.tensor_tensor(
-                out=part[t, "terms"][:, 0, planes],
+                out=part[t, 8][:, 0, planes],
                 in0=logits[t][:, planes, columns_of(t)],
                 in1=part[t, "max1"][:].unsqueeze(1).to_broadcast([P, BLOCK, P]),
                 op=ALU.subtract,
@@ -245,118 +244,118 @@ def tile_tokenlevelcompressor_pa_kernel(
         def exponentials(t, planes):
             if not live(t):
                 return
-            terms = part[t, "terms"]
+            terms = part[t, 8]
             nc.scalar.activation(out=terms[:, 0, planes], in_=terms[:, 0, planes], func=ACT.Exp)
 
         def products(t, planes):
             if not live(t):
                 return
-            terms = part[t, "terms"]
+            terms = part[t, 8]
             values = values_b[t][:, :, columns_of(t)] if planes == B_PLANES else acc[t, C_A][:]
             nc.vector.tensor_mul(out=terms[:, 1, planes], in0=terms[:, 0, planes], in1=values)
 
-        def sum_of_8(t):
-            if not live(t):
-                return
-            terms = part[t, "terms"]
-            part[t, "sum4"] = work.tile([P, 2, 4, P], F32, name="sum4")
-            nc.vector.tensor_add(out=part[t, "sum4"][:], in0=terms[:, :, 0:4], in1=terms[:, :, 4:8])
+        def planes_left(t):
+            return PLANES_LEFT_AT_THE_END if t >= TILES - TILES_AT_THE_END else PLANES_LEFT
 
-        def sum_of_4(t):
-            if not live(t):
+        def halve(t, planes):
+            if not live(t) or planes_left(t) >= planes:
                 return
-            sum4 = part[t, "sum4"]
-            part[t, "sum2"] = work.tile([P, 2, 2, P], F32, name="sum2")
-            nc.vector.tensor_add(out=part[t, "sum2"][:], in0=sum4[:, :, 0:2], in1=sum4[:, :, 2:4])
+            half = planes // 2
+            part[t, half] = work.tile([P, 2, half, P], F32, name="sum%d" % half)
+            nc.vector.tensor_add(
+                out=part[t, half][:], in0=part[t, planes][:, :, 0:half], in1=part[t, planes][:, :, half:planes]
+            )
 
-        def sum_of_2(t):
+        def window_sums(t):
             if not live(t):
                 return
-            sum2 = part[t, "sum2"]
-            part[t, "sum1"] = work.tile([P, 2, P], F32, name="sum1")
-            nc.vector.tensor_add(out=part[t, "sum1"][:], in0=sum2[:, :, 0], in1=sum2[:, :, 1])
+            planes = planes_left(t)
+            bank = psum_t.tile([P, 2, 2, P], F32, name="bank")
+            part[t, "sums"] = bank
+            for kind in range(2):
+                for entry in range(planes):
+                    nc.tensor.matmul(
+                        out=bank[:, 0, kind, :],
+                        lhsT=part[t, planes][:, kind, entry, :],
+                        rhs=ident[:],
+                        is_transpose=True,
+                        start=(entry == 0),
+                        stop=(entry == planes - 1),
+                    )
 
         def invert(t):
             if not live(t):
                 return
-            part[t, "inverse"] = work.tile([P, P], F32, name="inverse")
-            nc.vector.reciprocal(out=part[t, "inverse"][:], in_=part[t, "sum1"][:, 0])
+            part[t, "inverse"] = work.tile([P, FEATURES], F32, name="inverse")
+            nc.vector.reciprocal(out=part[t, "inverse"][:], in_=part[t, "sums"][:, 0, 0, :])
 
         def normalise(t):
             if not live(t):
                 return
-            part[t, "result"] = work.tile([P, P], F32, name="result")
+            part[t, "result"] = work.tile([P, FEATURES], F32, name="result")
             nc.vector.tensor_mul(
-                out=part[t, "result"][:], in0=part[t, "sum1"][:, 1], in1=part[t, "inverse"][:]
+                out=part[t, "result"][:], in0=part[t, "sums"][:, 0, 1, :], in1=part[t, "inverse"][:]
             )
 
         def store(t):
             if not live(t):
                 return
-            bank = psum_t.tile([P, 2, 2, P], F32, name="bank")
-            nc.tensor.transpose(bank[:, 0, 0, :], part[t, "result"][:], ident[:])
-            rows = work.tile([P, FEATURES], F32, name="out_rows")
-            nc.scalar.copy(out=rows[:], in_=bank[:, 0, 0, :])
-            nc.scalar.dma_start(out=out_tiles[t], in_=rows[:])
+            nc.sync.dma_start(out=out_tiles[t], in_=part[t, "result"][:])
 
         with tc.manual_schedule():
             nc.vector.memset(w_scales[:].rearrange("p a g n -> p (a g n)").bitcast(I32), 0)
             make_identity(nc, ident[:])
             load_bias()
             load_h(0, 0, 0)
-            load_h(0, 0, 1)
             load_h(0, 1, 0)
+            load_h(0, 0, 1)
             load_h(0, 1, 1)
-            load_codes(Z_B)
-            load_codes(Z_A)
             load_h(1, 0, 0)
+            load_codes(Z_B)
+            load_h(1, 1, 0)
+            load_codes(Z_A)
             load_h(1, 0, 1)
             load_codes(C_B)
-            load_codes(C_A)
-            load_h(1, 1, 0)
             load_h(1, 1, 1)
+            load_codes(C_A)
             for a in (Z_B, Z_A, C_B, C_A):
                 load_scales(a)
 
-            for s in range(TILES + 3):
-                for pair in range(2):
-                    for half in range(2):
+            for s in range(TILES + 2):
+                for half in range(2):
+                    for pair in range(2):
                         load_h(s + 2, pair, half)
                 open_sequence(s - 1)
-                store(s - 3)
-                transpose_quarter(s, 0, 0)
+                transpose_pass(s, 0)
+                transpose_pass(s, 1)
                 project(s - 1, Z_B)
                 add_bias_b(s - 1)
-                transpose_quarter(s, 0, 1)
                 project(s - 1, Z_A)
                 add_bias_a(s - 1)
 
                 products(s - 2, B_PLANES)
                 products(s - 2, A_PLANES)
-                sum_of_8(s - 2)
-                quantise(s, 0, 0)
-                sum_of_4(s - 2)
-                quantise(s, 0, 1)
-                sum_of_2(s - 2)
-                quantise(s, 0, 2)
-                invert(s - 2)
-                quantise(s, 0, 3)
-                normalise(s - 2)
+                halve(s - 2, 8)
+                quantise(s, 0)
+                halve(s - 2, 4)
+                quantise(s, 1)
 
-                transpose_quarter(s, 1, 0)
+                window_sums(s - 2)
+                transpose_pass(s, 2)
+                transpose_pass(s, 3)
                 project(s - 1, C_B)
                 shift_values_b(s - 1)
-                transpose_quarter(s, 1, 1)
                 project(s - 1, C_A)
 
                 max_of_8(s - 1)
-                quantise(s, 1, 0)
+                invert(s - 2)
                 max_of_4(s - 1)
-                quantise(s, 1, 1)
+                normalise(s - 2)
                 max_of_2(s - 1)
+                quantise(s, 2)
                 subtract_max(s - 1, B_PLANES)
                 subtract_max(s - 1, A_PLANES)
-                quantise(s, 1, 2)
-                quantise(s, 1, 3)
+                store(s - 2)
+                quantise(s, 3)
                 exponentials(s - 1, B_PLANES)
                 exponentials(s - 1, A_PLANES)

@@ -327,9 +327,9 @@ def tile_tokenlevelcompressor_pa_kernel(
                         load_h(s + 2, pair, half)
                 open_sequence(s - 1)
                 transpose_pass(s, 0)
-                transpose_pass(s, 1)
                 project(s - 1, Z_B)
                 add_bias_b(s - 1)
+                transpose_pass(s, 1)
                 project(s - 1, Z_A)
                 add_bias_a(s - 1)
 
@@ -342,9 +342,9 @@ def tile_tokenlevelcompressor_pa_kernel(
 
                 window_sums(s - 2)
                 transpose_pass(s, 2)
-                transpose_pass(s, 3)
                 project(s - 1, C_B)
                 shift_values_b(s - 1)
+                transpose_pass(s, 3)
                 project(s - 1, C_A)
 
                 max_of_8(s - 1)

@@ -26,6 +26,7 @@ Z_B, Z_A, C_B, C_A = 0, 1, 2, 3
 B_PLANES, A_PLANES = slice(0, BLOCK), slice(BLOCK, 2 * BLOCK)
 
 PLANES_LEFT, PLANES_LEFT_AT_THE_END, TILES_AT_THE_END = 2, 8, 2
+WARM_UP = 6
 FLOPS = 2 * SEQS * SEQ_LEN * K * 4 * FEATURES
 
 
@@ -77,6 +78,7 @@ def tile_tokenlevelcompressor_pa_kernel(
         w_codes = const.tile([P, 4, PASSES, FEATURES], U32, align_bytes=64)
         w_scales = const.tile([P, 4, PASSES, FEATURES], U8, align_bytes=64)
         bias = const.tile([P, 2 * BLOCK], F32)
+        zeros = const.tile([P, TILE_TOKENS], BF16)
 
         def live(t):
             return 0 <= t < TILES
@@ -88,6 +90,16 @@ def tile_tokenlevelcompressor_pa_kernel(
         def shifted_columns_of(t):
             first = P * (t % TILES_PER_SEQ) + 1
             return slice(first, first + P)
+
+        def keep_warm(count):
+            for repeat in range(count):
+                nc.tensor.matmul(
+                    out=idle_bank[:].rearrange("p i j -> p (i j)"),
+                    lhsT=zeros[:, 0:P],
+                    rhs=zeros[:],
+                    start=True,
+                    stop=True,
+                )
 
         def load_h(t, pair, half):
             if not live(t):
@@ -120,6 +132,9 @@ def tile_tokenlevelcompressor_pa_kernel(
             nc.sync.dma_start(out=rows_bf16[BLOCK : 2 * BLOCK, :], in_=b_a)
             rows = const.tile([P, P], F32)
             nc.vector.tensor_copy(out=rows[:], in_=rows_bf16[:])
+            return rows
+
+        def turn_bias(rows):
             columns = psum_t.tile([P, 2, 2, P], F32, name="bank")
             nc.tensor.transpose(columns[:, 0, 0, :], rows[:], ident[:])
             nc.vector.tensor_copy(out=bias[:], in_=columns[:, 0, 0, 0 : 2 * BLOCK])
@@ -303,13 +318,16 @@ def tile_tokenlevelcompressor_pa_kernel(
             nc.sync.dma_start(out=out_tiles[t], in_=part[t, "result"][:])
 
         with tc.manual_schedule():
-            nc.vector.memset(w_scales[:].rearrange("p a g n -> p (a g n)").bitcast(I32), 0)
-            make_identity(nc, ident[:])
-            load_bias()
             load_h(0, 0, 0)
             load_h(0, 1, 0)
             load_h(0, 0, 1)
             load_h(0, 1, 1)
+            nc.vector.memset(zeros[:], 0.0)
+            idle_bank = psum_acc.tile([P, BLOCK, P], F32, name="acc")
+            keep_warm(WARM_UP)
+            make_identity(nc, ident[:])
+            nc.vector.memset(w_scales[:].rearrange("p a g n -> p (a g n)").bitcast(I32), 0)
+            bias_rows = load_bias()
             load_h(1, 0, 0)
             load_codes(Z_B)
             load_h(1, 1, 0)
@@ -327,9 +345,14 @@ def tile_tokenlevelcompressor_pa_kernel(
                         load_h(s + 2, pair, half)
                 open_sequence(s - 1)
                 transpose_pass(s, 0)
+                if s == 0:
+                    turn_bias(bias_rows)
+                    keep_warm(1)
                 project(s - 1, Z_B)
                 add_bias_b(s - 1)
                 transpose_pass(s, 1)
+                if s == 0:
+                    keep_warm(1)
                 project(s - 1, Z_A)
                 add_bias_a(s - 1)
 
@@ -342,9 +365,13 @@ def tile_tokenlevelcompressor_pa_kernel(
 
                 window_sums(s - 2)
                 transpose_pass(s, 2)
+                if s == 0:
+                    keep_warm(1)
                 project(s - 1, C_B)
                 shift_values_b(s - 1)
                 transpose_pass(s, 3)
+                if s == 0:
+                    keep_warm(1)
                 project(s - 1, C_A)
 
                 max_of_8(s - 1)

@@ -63,7 +63,8 @@ def tile_tokenlevelcompressor_pa_kernel(
         seq_pool = ctx.enter_context(tc.tile_pool(name="seq", bufs=2))
         work = ctx.enter_context(tc.tile_pool(name="work", bufs=2))
         psum_t = ctx.enter_context(tc.psum_pool(name="psum_t", bufs=4))
-        psum_acc = ctx.enter_context(tc.psum_pool(name="psum_acc", bufs=4))
+        psum_acc = ctx.enter_context(tc.psum_pool(name="psum_acc", bufs=3))
+        psum_sums = ctx.enter_context(tc.psum_pool(name="psum_sums", bufs=1))
 
         h_sb = {}
         grouped = {}
@@ -285,7 +286,7 @@ def tile_tokenlevelcompressor_pa_kernel(
             if not live(t):
                 return
             planes = planes_left(t)
-            bank = psum_t.tile([P, 2, 2, P], F32, name="bank")
+            bank = psum_sums.tile([P, 2, 2, P], F32, name="sums")
             part[t, "sums"] = bank
             for kind in range(2):
                 for entry in range(planes):
@@ -363,26 +364,26 @@ def tile_tokenlevelcompressor_pa_kernel(
                 halve(s - 2, 4)
                 quantise(s, 1)
 
-                window_sums(s - 2)
                 transpose_pass(s, 2)
                 if s == 0:
                     keep_warm(1)
                 project(s - 1, C_B)
                 shift_values_b(s - 1)
+                window_sums(s - 2)
                 transpose_pass(s, 3)
                 if s == 0:
                     keep_warm(1)
                 project(s - 1, C_A)
 
                 max_of_8(s - 1)
-                invert(s - 2)
                 max_of_4(s - 1)
-                normalise(s - 2)
                 max_of_2(s - 1)
                 quantise(s, 2)
                 subtract_max(s - 1, B_PLANES)
                 subtract_max(s - 1, A_PLANES)
-                store(s - 2)
+                invert(s - 2)
                 quantise(s, 3)
+                normalise(s - 2)
+                store(s - 2)
                 exponentials(s - 1, B_PLANES)
                 exponentials(s - 1, A_PLANES)

@@ -25,7 +25,7 @@ NEG = -3.4028234663852886e38
 Z_B, Z_A, C_B, C_A = 0, 1, 2, 3
 B_PLANES, A_PLANES = slice(0, BLOCK), slice(BLOCK, 2 * BLOCK)
 
-PLANES_LEFT, PLANES_LEFT_AT_THE_END, TILES_AT_THE_END = 2, 8, 2
+PLANES_LEFT, PLANES_LEFT_AT_THE_END, TILES_AT_THE_END = 1, 8, 2
 WARM_UP = 6
 FLOPS = 2 * SEQS * SEQ_LEN * K * 4 * FEATURES
 
@@ -219,26 +219,25 @@ def tile_tokenlevelcompressor_pa_kernel(
                     bias=bias[:, BLOCK + i : BLOCK + i + 1],
                 )
 
-        def max_of_8(t):
+        def max_of_4(t, planes, name):
             if not live(t):
                 return
-            mine = logits[t][:, :, columns_of(t)]
-            part[t, "max4"] = work.tile([P, 4, P], F32, name="max4")
-            nc.vector.tensor_max(out=part[t, "max4"][:], in0=mine[:, 0:4], in1=mine[:, 4:8])
+            mine = logits[t][:, planes, columns_of(t)]
+            part[t, name, 2] = work.tile([P, 2, P], F32, name=name + "2")
+            nc.vector.tensor_max(out=part[t, name, 2][:], in0=mine[:, 0:2], in1=mine[:, 2:4])
 
-        def max_of_4(t):
+        def max_of_2(t, name):
             if not live(t):
                 return
-            max4 = part[t, "max4"]
-            part[t, "max2"] = work.tile([P, 2, P], F32, name="max2")
-            nc.vector.tensor_max(out=part[t, "max2"][:], in0=max4[:, 0:2], in1=max4[:, 2:4])
+            two = part[t, name, 2]
+            part[t, name, 1] = work.tile([P, P], F32, name=name + "1")
+            nc.vector.tensor_max(out=part[t, name, 1][:], in0=two[:, 0], in1=two[:, 1])
 
-        def max_of_2(t):
+        def max_of_branches(t):
             if not live(t):
                 return
-            max2 = part[t, "max2"]
             part[t, "max1"] = work.tile([P, P], F32, name="max1")
-            nc.vector.tensor_max(out=part[t, "max1"][:], in0=max2[:, 0], in1=max2[:, 1])
+            nc.vector.tensor_max(out=part[t, "max1"][:], in0=part[t, "b", 1][:], in1=part[t, "a", 1][:])
 
         def subtract_max(t, planes):
             if not live(t):
@@ -286,7 +285,10 @@ def tile_tokenlevelcompressor_pa_kernel(
             if not live(t):
                 return
             planes = planes_left(t)
-            bank = psum_sums.tile([P, 2, 2, P], F32, name="sums")
+            if t >= TILES - TILES_AT_THE_END:
+                bank = psum_t.tile([P, 2, 2, P], F32, name="bank")
+            else:
+                bank = psum_sums.tile([P, 2, 2, P], F32, name="sums")
             part[t, "sums"] = bank
             for kind in range(2):
                 for entry in range(planes):
@@ -318,6 +320,14 @@ def tile_tokenlevelcompressor_pa_kernel(
                 return
             nc.sync.dma_start(out=out_tiles[t], in_=part[t, "result"][:])
 
+        def turn(k):
+            transpose_pass(k // PASSES, k % PASSES)
+            if k <= PASSES:
+                keep_warm(1)
+
+        def pack(k):
+            quantise(k // PASSES, k % PASSES)
+
         with tc.manual_schedule():
             load_h(0, 0, 0)
             load_h(0, 1, 0)
@@ -340,50 +350,59 @@ def tile_tokenlevelcompressor_pa_kernel(
             for a in (Z_B, Z_A, C_B, C_A):
                 load_scales(a)
 
+            turn(0)
+            turn_bias(bias_rows)
+            pack(0)
             for s in range(TILES + 2):
+                first = PASSES * s + 1
+                at_the_end = s >= TILES
                 for half in range(2):
                     for pair in range(2):
                         load_h(s + 2, pair, half)
                 open_sequence(s - 1)
-                transpose_pass(s, 0)
-                if s == 0:
-                    turn_bias(bias_rows)
-                    keep_warm(1)
+                turn(first)
                 project(s - 1, Z_B)
                 add_bias_b(s - 1)
-                transpose_pass(s, 1)
-                if s == 0:
-                    keep_warm(1)
+                turn(first + 1)
                 project(s - 1, Z_A)
                 add_bias_a(s - 1)
 
                 products(s - 2, B_PLANES)
                 products(s - 2, A_PLANES)
+                if at_the_end:
+                    window_sums(s - 2)
                 halve(s - 2, 8)
-                quantise(s, 0)
+                pack(first)
                 halve(s - 2, 4)
-                quantise(s, 1)
+                max_of_4(s - 1, B_PLANES, "b")
+                halve(s - 2, 2)
+                max_of_2(s - 1, "b")
+                pack(first + 1)
 
-                transpose_pass(s, 2)
-                if s == 0:
-                    keep_warm(1)
+                turn(first + 2)
                 project(s - 1, C_B)
                 shift_values_b(s - 1)
-                window_sums(s - 2)
-                transpose_pass(s, 3)
-                if s == 0:
-                    keep_warm(1)
+                if not at_the_end:
+                    window_sums(s - 2)
+                turn(first + 3)
                 project(s - 1, C_A)
 
-                max_of_8(s - 1)
-                max_of_4(s - 1)
-                max_of_2(s - 1)
-                quantise(s, 2)
+                max_of_4(s - 1, A_PLANES, "a")
+                if at_the_end:
+                    invert(s - 2)
+                max_of_2(s - 1, "a")
+                if at_the_end:
+                    normalise(s - 2)
+                    store(s - 2)
+                max_of_branches(s - 1)
+                pack(first + 2)
                 subtract_max(s - 1, B_PLANES)
                 subtract_max(s - 1, A_PLANES)
-                invert(s - 2)
-                quantise(s, 3)
-                normalise(s - 2)
-                store(s - 2)
+                if not at_the_end:
+                    invert(s - 2)
+                pack(first + 3)
+                if not at_the_end:
+                    normalise(s - 2)
+                    store(s - 2)
                 exponentials(s - 1, B_PLANES)
                 exponentials(s - 1, A_PLANES)

@@ -117,13 +117,13 @@ def tile_tokenlevelcompressor_pa_kernel(
                 in_=weights[a][0].rearrange("g p n t -> p g (n t)").bitcast(I32),
             )
 
-        def load_scales(a):
+        def load_scales(a, queue, view):
             for quadrant in range(4):
-                nc.gpsimd.dma_start(
-                    out=w_scales[32 * quadrant : 32 * quadrant + 4, a].bitcast(F32),
+                queue.dma_start(
+                    out=w_scales[32 * quadrant : 32 * quadrant + 4, a].bitcast(view),
                     in_=weights[a][1][:, 4 * quadrant : 4 * quadrant + 4, :]
                     .rearrange("g r n -> r g n")
-                    .bitcast(F32),
+                    .bitcast(view),
                 )
 
         def load_bias():
@@ -347,8 +347,10 @@ def tile_tokenlevelcompressor_pa_kernel(
             load_codes(C_B)
             load_h(1, 1, 1)
             load_codes(C_A)
-            for a in (Z_B, Z_A, C_B, C_A):
-                load_scales(a)
+            load_scales(Z_B, nc.gpsimd, F32)
+            load_scales(Z_A, nc.gpsimd, F32)
+            load_scales(C_B, nc.sync, I32)
+            load_scales(C_A, nc.sync, I32)
 
             turn(0)
             turn_bias(bias_rows)

@@ -269,6 +269,9 @@ def tile_tokenlevelcompressor_pa_kernel(
             values = values_b[t][:, :, columns_of(t)] if planes == B_PLANES else acc[t, C_A][:]
             nc.vector.tensor_mul(out=terms[:, 1, planes], in0=terms[:, 0, planes], in1=values)
 
+        def in_the_stream(t):
+            return 0 <= t < TILES - TILES_AT_THE_END
+
         def planes_left(t):
             return PLANES_LEFT_AT_THE_END if t >= TILES - TILES_AT_THE_END else PLANES_LEFT
 
@@ -384,8 +387,8 @@ def tile_tokenlevelcompressor_pa_kernel(
                 turn(first + 2)
                 project(s - 1, C_B)
                 shift_values_b(s - 1)
-                if not at_the_end:
-                    window_sums(s - 2)
+                if in_the_stream(s - 3):
+                    window_sums(s - 3)
                 turn(first + 3)
                 project(s - 1, C_A)
 
@@ -400,11 +403,11 @@ def tile_tokenlevelcompressor_pa_kernel(
                 pack(first + 2)
                 subtract_max(s - 1, B_PLANES)
                 subtract_max(s - 1, A_PLANES)
-                if not at_the_end:
-                    invert(s - 2)
+                if in_the_stream(s - 3):
+                    invert(s - 3)
                 pack(first + 3)
-                if not at_the_end:
-                    normalise(s - 2)
-                    store(s - 2)
+                if in_the_stream(s - 3):
+                    normalise(s - 3)
+                    store(s - 3)
                 exponentials(s - 1, B_PLANES)
                 exponentials(s - 1, A_PLANES)

from contextlib import ExitStack

import concourse.mybir as mybir
from concourse.masks import make_identity

F32 = mybir.dt.float32
BF16 = mybir.dt.bfloat16
I32 = mybir.dt.int32
U32 = mybir.dt.uint32
U8 = mybir.dt.uint8
FP8X4 = mybir.dt.float8_e4m3fn_x4
ALU = mybir.AluOpType
ACT = mybir.ActivationFunctionType

P = 128
SEQS, SEQ_LEN, K, FEATURES, BLOCK = 4, 1024, 2048, 128, 4
K_PASS = 4 * P
PASSES = K // K_PASS
WORDS = K_PASS // 2
TILE_TOKENS = BLOCK * P
TILES = SEQS * SEQ_LEN // TILE_TOKENS
TILES_PER_SEQ = SEQ_LEN // TILE_TOKENS
PLANE = SEQ_LEN // BLOCK + 8
NEG = -3.4028234663852886e38
Z_B, Z_A, C_B, C_A = 0, 1, 2, 3
B_PLANES, A_PLANES = slice(0, BLOCK), slice(BLOCK, 2 * BLOCK)

PLANES_LEFT, PLANES_LEFT_AT_THE_END, TILES_AT_THE_END = 1, 8, 2
WARM_UP = 6
FLOPS = 2 * SEQS * SEQ_LEN * K * 4 * FEATURES


def tile_tokenlevelcompressor_pa_kernel(
    tc,
    h,
    w_kv_a_words,
    w_kv_a_scales,
    w_kv_b_words,
    w_kv_b_scales,
    w_z_a_words,
    w_z_a_scales,
    w_z_b_words,
    w_z_b_scales,
    b_a,
    b_b,
    out,
):
    nc = tc.nc
    weights = {
        Z_B: (w_z_b_words, w_z_b_scales),
        Z_A: (w_z_a_words, w_z_a_scales),
        C_B: (w_kv_b_words, w_kv_b_scales),
        C_A: (w_kv_a_words, w_kv_a_scales),
    }
    h_tiles = h.flatten_outer_dims().rearrange("(t p i) k -> t p i k", p=P, i=BLOCK)
    out_tiles = out.flatten_outer_dims().rearrange("(t p) f -> t p f", p=P)

    with ExitStack() as ctx:
        const = ctx.enter_context(tc.tile_pool(name="const", bufs=1))
        h_pool = ctx.enter_context(tc.tile_pool(name="h", bufs=12))
        grouped_pool = ctx.enter_context(tc.tile_pool(name="grouped", bufs=4))
        mx_pool = ctx.enter_context(tc.tile_pool(name="mx", bufs=3))
        seq_pool = ctx.enter_context(tc.tile_pool(name="seq", bufs=2))
        work = ctx.enter_context(tc.tile_pool(name="work", bufs=2))
        psum_t = ctx.enter_context(tc.psum_pool(name="psum_t", bufs=4))
        psum_acc = ctx.enter_context(tc.psum_pool(name="psum_acc", bufs=3))
        psum_sums = ctx.enter_context(tc.psum_pool(name="psum_sums", bufs=1))

        h_sb = {}
        grouped = {}
        codes = {}
        scales = {}
        acc = {}
        logits = {}
        values_b = {}
        part = {}

        ident = const.tile([P, P], F32)
        w_codes = const.tile([P, 4, PASSES, FEATURES], U32, align_bytes=64)
        w_scales = const.tile([P, 4, PASSES, FEATURES], U8, align_bytes=64)
        bias = const.tile([P, 2 * BLOCK], F32)
        zeros = const.tile([P, TILE_TOKENS], BF16)

        def live(t):
            return 0 <= t < TILES

        def columns_of(t):
            first = P * (t % TILES_PER_SEQ)
            return slice(first, first + P)

        def shifted_columns_of(t):
            first = P * (t % TILES_PER_SEQ) + 1
            return slice(first, first + P)

        def keep_warm(count):
            for repeat in range(count):
                nc.tensor.matmul(
                    out=idle_bank[:].rearrange("p i j -> p (i j)"),
                    lhsT=zeros[:, 0:P],
                    rhs=zeros[:],
                    start=True,
                    stop=True,
                )

        def load_h(t, pair, half):
            if not live(t):
                return
            h_sb[t, pair, half] = h_pool.tile([P, 2, K // 2], BF16, name="h_sb")
            nc.sync.dma_start(
                out=h_sb[t, pair, half][:],
                in_=h_tiles[t][:, 2 * pair : 2 * pair + 2, (K // 2) * half : (K // 2) * (half + 1)],
            )

        def load_codes(a):
            nc.sync.dma_start(
                out=w_codes[:, a].bitcast(I32),
                in_=weights[a][0].rearrange("g p n t -> p g (n t)").bitcast(I32),
            )

        def load_scales(a, queue, view):
            for quadrant in range(4):
                queue.dma_start(
                    out=w_scales[32 * quadrant : 32 * quadrant + 4, a].bitcast(view),
                    in_=weights[a][1][:, 4 * quadrant : 4 * quadrant + 4, :]
                    .rearrange("g r n -> r g n")
                    .bitcast(view),
                )

        def load_bias():
            rows_bf16 = const.tile([P, P], BF16)
            nc.vector.memset(rows_bf16[:], 0.0)
            nc.sync.dma_start(out=rows_bf16[0:BLOCK, :], in_=b_b)
            nc.sync.dma_start(out=rows_bf16[BLOCK : 2 * BLOCK, :], in_=b_a)
            rows = const.tile([P, P], F32)
            nc.vector.tensor_copy(out=rows[:], in_=rows_bf16[:])
            return rows

        def turn_bias(rows):
            columns = psum_t.tile([P, 2, 2, P], F32, name="bank")
            nc.tensor.transpose(columns[:, 0, 0, :], rows[:], ident[:])
            nc.vector.tensor_copy(out=bias[:], in_=columns[:, 0, 0, 0 : 2 * BLOCK])

        def transpose_pass(t, g):
            if not live(t):
                return
            grouped[t, g] = grouped_pool.tile([P, BLOCK, P, 4], BF16, name="grouped", align_bytes=64)
            for pair in range(2):
                h_words = h_sb[t, pair, g // 2][:].bitcast(F32)
                first = WORDS * (g % 2)
                bank = psum_t.tile([P, 2, 2, P], F32, name="bank")
                for i in range(2):
                    for u in range(2):
                        nc.tensor.transpose(
                            bank[:, i, u, :], h_words[:, i, first + u : first + WORDS : 2], ident[:]
                        )
                nc.scalar.copy(
                    out=grouped[t, g][:, 2 * pair : 2 * pair + 2].bitcast(F32),
                    in_=bank[:].rearrange("p i u c -> p i c u"),
                )

        def quantise(t, g):
            if not live(t):
                return
            if g == 0:
                codes[t] = mx_pool.tile([P, PASSES, BLOCK, P], U32, name="codes", align_bytes=64)
                scales[t] = mx_pool.tile([P, PASSES, BLOCK, P], U8, name="scales", align_bytes=64)
            nc.vector.quantize_mx(
                out=codes[t][:, g].rearrange("p i c -> p (i c)").bitcast(FP8X4),
                scales=scales[t][:, g].rearrange("p i c -> p (i c)"),
                in_=grouped[t, g][:].rearrange("p i c t -> p (i c t)"),
            )

        def project(t, a):
            if not live(t):
                return
            acc[t, a] = psum_acc.tile([P, BLOCK, P], F32, name="acc")
            for g in range(PASSES):
                nc.tensor.matmul_mx(
                    out=acc[t, a][:].rearrange("p i j -> p (i j)"),
                    lhsT=w_codes[:, a, g, :].bitcast(FP8X4),
                    lhsT_scale=w_scales[:, a, g, :],
                    rhs=codes[t][:, g].rearrange("p i c -> p (i c)").bitcast(FP8X4),
                    rhs_scale=scales[t][:, g].rearrange("p i c -> p (i c)"),
                    start=(g == 0),
                    stop=(g == PASSES - 1),
                )

        def open_sequence(t):
            if not live(t):
                return
            if t % TILES_PER_SEQ != 0:
                logits[t] = logits[t - 1]
                values_b[t] = values_b[t - 1]
                return
            logits[t] = seq_pool.tile([P, 2 * BLOCK, PLANE], F32, name="logits")
            values_b[t] = seq_pool.tile([P, BLOCK, PLANE], F32, name="values_b")
            nc.vector.memset(logits[t][:, 0:BLOCK, 0:8], NEG)
            nc.vector.memset(values_b[t][:, :, 0:8], 0.0)

        def add_bias_b(t):
            if not live(t):
                return
            for i in range(BLOCK):
                nc.scalar.activation(
                    out=logits[t][:, i, shifted_columns_of(t)],
                    in_=acc[t, Z_B][:, i, :],
                    func=ACT.Identity,
                    bias=bias[:, i : i + 1],
                )

        def add_bias_a(t):
            if not live(t):
                return
            for i in range(BLOCK):
                nc.scalar.activation(
                    out=logits[t][:, BLOCK + i, columns_of(t)],
                    in_=acc[t, Z_A][:, i, :],
                    func=ACT.Identity,
                    bias=bias[:, BLOCK + i : BLOCK + i + 1],
                )

        def max_of_4(t, planes, name):
            if not live(t):
                return
            mine = logits[t][:, planes, columns_of(t)]
            part[t, name, 2] = work.tile([P, 2, P], F32, name=name + "2")
            nc.vector.tensor_max(out=part[t, name, 2][:], in0=mine[:, 0:2], in1=mine[:, 2:4])

        def max_of_2(t, name):
            if not live(t):
                return
            two = part[t, name, 2]
            part[t, name, 1] = work.tile([P, P], F32, name=name + "1")
            nc.vector.tensor_max(out=part[t, name, 1][:], in0=two[:, 0], in1=two[:, 1])

        def max_of_branches(t):
            if not live(t):
                return
            part[t, "max1"] = work.tile([P, P], F32, name="max1")
            nc.vector.tensor_max(out=part[t, "max1"][:], in0=part[t, "b", 1][:], in1=part[t, "a", 1][:])

        def subtract_max(t, planes):
            if not live(t):
                return
            if planes == B_PLANES:
                part[t, 8] = work.tile([P, 2, 2 * BLOCK, P], F32, name="terms")
            nc.vector.tensor_tensor(
                out=part[t, 8][:, 0, planes],
                in0=logits[t][:, planes, columns_of(t)],
                in1=part[t, "max1"][:].unsqueeze(1).to_broadcast([P, BLOCK, P]),
                op=ALU.subtract,
            )

        def shift_values_b(t):
            if not live(t):
                return
            nc.scalar.copy(out=values_b[t][:, :, shifted_columns_of(t)], in_=acc[t, C_B][:])

        def exponentials(t, planes):
            if not live(t):
                return
            terms = part[t, 8]
            nc.scalar.activation(out=terms[:, 0, planes], in_=terms[:, 0, planes], func=ACT.Exp)

        def products(t, planes):
            if not live(t):
                return
            terms = part[t, 8]
            values = values_b[t][:, :, columns_of(t)] if planes == B_PLANES else acc[t, C_A][:]
            nc.vector.tensor_mul(out=terms[:, 1, planes], in0=terms[:, 0, planes], in1=values)

        def in_the_stream(t):
            return 0 <= t < TILES - TILES_AT_THE_END

        def planes_left(t):
            return PLANES_LEFT_AT_THE_END if t >= TILES - TILES_AT_THE_END else PLANES_LEFT

        def halve(t, planes):
            if not live(t) or planes_left(t) >= planes:
                return
            half = planes // 2
            part[t, half] = work.tile([P, 2, half, P], F32, name="sum%d" % half)
            nc.vector.tensor_add(
                out=part[t, half][:], in0=part[t, planes][:, :, 0:half], in1=part[t, planes][:, :, half:planes]
            )

        def window_sums(t):
            if not live(t):
                return
            planes = planes_left(t)
            if t >= TILES - TILES_AT_THE_END:
                bank = psum_t.tile([P, 2, 2, P], F32, name="bank")
            else:
                bank = psum_sums.tile([P, 2, 2, P], F32, name="sums")
            part[t, "sums"] = bank
            for kind in range(2):
                for entry in range(planes):
                    nc.tensor.matmul(
                        out=bank[:, 0, kind, :],
                        lhsT=part[t, planes][:, kind, entry, :],
                        rhs=ident[:],
                        is_transpose=True,
                        start=(entry == 0),
                        stop=(entry == planes - 1),
                    )

        def invert(t):
            if not live(t):
                return
            part[t, "inverse"] = work.tile([P, FEATURES], F32, name="inverse")
            nc.vector.reciprocal(out=part[t, "inverse"][:], in_=part[t, "sums"][:, 0, 0, :])

        def normalise(t):
            if not live(t):
                return
            part[t, "result"] = work.tile([P, FEATURES], F32, name="result")
            nc.vector.tensor_mul(
                out=part[t, "result"][:], in0=part[t, "sums"][:, 0, 1, :], in1=part[t, "inverse"][:]
            )

        def store(t):
            if not live(t):
                return
            nc.sync.dma_start(out=out_tiles[t], in_=part[t, "result"][:])

        def turn(k):
            transpose_pass(k // PASSES, k % PASSES)
            if k <= PASSES:
                keep_warm(1)

        def pack(k):
            quantise(k // PASSES, k % PASSES)

        with tc.manual_schedule():
            load_h(0, 0, 0)
            load_h(0, 1, 0)
            load_h(0, 0, 1)
            load_h(0, 1, 1)
            nc.vector.memset(zeros[:], 0.0)
            idle_bank = psum_acc.tile([P, BLOCK, P], F32, name="acc")
            keep_warm(WARM_UP)
            make_identity(nc, ident[:])
            nc.vector.memset(w_scales[:].rearrange("p a g n -> p (a g n)").bitcast(I32), 0)
            bias_rows = load_bias()
            load_h(1, 0, 0)
            load_codes(Z_B)
            load_h(1, 1, 0)
            load_codes(Z_A)
            load_h(1, 0, 1)
            load_codes(C_B)
            load_h(1, 1, 1)
            load_codes(C_A)
            load_scales(Z_B, nc.gpsimd, F32)
            load_scales(Z_A, nc.gpsimd, F32)
            load_scales(C_B, nc.sync, I32)
            load_scales(C_A, nc.sync, I32)

            turn(0)
            turn_bias(bias_rows)
            pack(0)
            for s in range(TILES + 2):
                first = PASSES * s + 1
                at_the_end = s >= TILES
                for half in range(2):
                    for pair in range(2):
                        load_h(s + 2, pair, half)
                open_sequence(s - 1)
                turn(first)
                project(s - 1, Z_B)
                add_bias_b(s - 1)
                turn(first + 1)
                project(s - 1, Z_A)
                add_bias_a(s - 1)

                products(s - 2, B_PLANES)
                products(s - 2, A_PLANES)
                if at_the_end:
                    window_sums(s - 2)
                halve(s - 2, 8)
                pack(first)
                halve(s - 2, 4)
                max_of_4(s - 1, B_PLANES, "b")
                halve(s - 2, 2)
                max_of_2(s - 1, "b")
                pack(first + 1)

                turn(first + 2)
                project(s - 1, C_B)
                shift_values_b(s - 1)
                if in_the_stream(s - 3):
                    window_sums(s - 3)
                turn(first + 3)
                project(s - 1, C_A)

                max_of_4(s - 1, A_PLANES, "a")
                if at_the_end:
                    invert(s - 2)
                max_of_2(s - 1, "a")
                if at_the_end:
                    normalise(s - 2)
                    store(s - 2)
                max_of_branches(s - 1)
                pack(first + 2)
                subtract_max(s - 1, B_PLANES)
                subtract_max(s - 1, A_PLANES)
                if in_the_stream(s - 3):
                    invert(s - 3)
                pack(first + 3)
                if in_the_stream(s - 3):
                    normalise(s - 3)
                    store(s - 3)
                exponentials(s - 1, B_PLANES)
                exponentials(s - 1, A_PLANES)
